import numpy as np
import ml_dtypes

BF16 = ml_dtypes.bfloat16


def bf(x):
    return np.asarray(x, np.float32).astype(BF16)


def f32(x):
    return np.asarray(x, np.float32)


def f64(x):
    return np.asarray(x).astype(np.float64)


def striped(idx):
    return np.tile(idx.reshape(-1, 16).T, (8, 1))


D, M, S, N = 128, 128, 2048, 1024


def setup_inputs():
    return {"table": bf(np.abs(np.random.standard_normal((D, S)))), "v": bf(0.05 * np.random.standard_normal((D, M))), "gain": f32(1.0 + 0.2 * np.random.standard_normal((M, 1))), "offs": striped(np.random.permutation(S)[:N])}


def reference(table, v, gain, offs):
    idx = offs[:16].T.reshape(-1)
    vv = f64(v)
    scale = f64(gain) / np.sqrt((vv * vv).sum(0))[:, None]
    return np.maximum(scale * (vv.T @ f64(table)[:, idx]), 0.0)

@@ -1,0 +1,53 @@
+import concourse.mybir as mybir
+
+BF16, F32, U16 = mybir.dt.bfloat16, mybir.dt.float32, mybir.dt.uint16
+MULT, MAX = mybir.AluOpType.mult, mybir.AluOpType.max
+SQRT, RELU = mybir.ActivationFunctionType.Sqrt, mybir.ActivationFunctionType.Relu
+
+K = 128
+M = 128
+S = 2048
+N = 1024
+PIECE = 512
+PER_COLUMN = 16
+
+FLOPS = 2 * K * M * N
+
+
+def tile_qnetwork_kernel(tc, table, v, gain, offs, out):
+    nc = tc.nc
+    with tc.tile_pool(name="held", bufs=1) as held, tc.psum_pool(name="psum", bufs=1) as psum:
+        offsets = held.tile([K, N // PER_COLUMN], U16, name="offsets")
+        nc.sync.dma_start(offsets[:], offs)
+        weights = held.tile([K, M], BF16, name="weights")
+        nc.scalar.dma_start(weights[:], v)
+        gain_col = held.tile([M, 1], F32, name="gain_col")
+        nc.scalar.dma_start(gain_col[:], gain)
+        nodes = held.tile([K, S], BF16, name="nodes")
+        nc.sync.dma_start(nodes[:], table)
+
+        squares = held.tile([K, M], F32, name="squares")
+        nc.vector.tensor_tensor(squares[:], weights[:], weights[:], MULT)
+        ones = held.tile([K, 1], F32, name="ones")
+        nc.vector.memset(ones[:], 1.0)
+        sum_squares = psum.tile([M, 1], F32, name="sum_squares")
+        nc.tensor.matmul(sum_squares[:], squares[:], ones[:], start=True, stop=True)
+        length = held.tile([M, 1], F32, name="length")
+        nc.scalar.activation(length[:], sum_squares[:], SQRT)
+        inverse_length = held.tile([M, 1], F32, name="inverse_length")
+        nc.vector.reciprocal(inverse_length[:], length[:])
+        scale = held.tile([M, 1], F32, name="scale")
+        nc.vector.tensor_tensor(scale[:], inverse_length[:], gain_col[:], MULT)
+
+        for piece in range(N // PIECE):
+            first = piece * PIECE
+            looked_up = nodes[:].indirect(offsets[:, first // PER_COLUMN : (first + PIECE) // PER_COLUMN])
+            projected = psum.tile([M, PIECE], F32, name=f"projected{piece}")
+            nc.tensor.matmul(projected[:], weights[:], looked_up, start=True, stop=True)
+            result = held.tile([M, PIECE], F32, name=f"result{piece}")
+            if piece % 2 == 0:
+                nc.scalar.activation(result[:], projected[:], RELU, scale=scale[:])
+                nc.sync.dma_start(out[:, first : first + PIECE], result[:])
+            else:
+                nc.vector.tensor_scalar(result[:], projected[:], scale[:], 0.0, MULT, MAX)
+                nc.scalar.dma_start(out[:, first : first + PIECE], result[:])

@@ -8,7 +8,7 @@ K = 128
 M = 128
 S = 2048
 N = 1024
-PIECE = 512
+PIECE = 256
 PER_COLUMN = 16
 
 FLOPS = 2 * K * M * N
@@ -47,7 +47,7 @@ def tile_qnetwork_kernel(tc, table, v, gain, offs, out):
             result = held.tile([M, PIECE], F32, name=f"result{piece}")
             if piece % 2 == 0:
                 nc.scalar.activation(result[:], projected[:], RELU, scale=scale[:])
-                nc.sync.dma_start(out[:, first : first + PIECE], result[:])
+                nc.scalar.dma_start(out[:, first : first + PIECE], result[:])
             else:
                 nc.vector.tensor_scalar(result[:], projected[:], scale[:], 0.0, MULT, MAX)
-                nc.scalar.dma_start(out[:, first : first + PIECE], result[:])
+                nc.sync.dma_start(out[:, first : first + PIECE], result[:])

@@ -11,6 +11,9 @@ N = 1024
 PIECE = 256
 PER_COLUMN = 16
 
+WARM_UP = 4
+BANK = 512
+
 FLOPS = 2 * K * M * N
 
 
@@ -25,6 +28,12 @@ def tile_qnetwork_kernel(tc, table, v, gain, offs, out):
         nc.scalar.dma_start(gain_col[:], gain)
         nodes = held.tile([K, S], BF16, name="nodes")
         nc.sync.dma_start(nodes[:], table)
+
+        zeros = held.tile([K, M], BF16, name="zeros")
+        nc.vector.memset(zeros[:], 0.0)
+        unread = psum.tile([M, BANK], F32, name="unread")
+        for turn in range(WARM_UP):
+            nc.tensor.matmul(unread[:], zeros[:], zeros[:, 0:1].to_broadcast([K, BANK]), start=True, stop=True)
 
         squares = held.tile([K, M], F32, name="squares")
         nc.vector.tensor_tensor(squares[:], weights[:], weights[:], MULT)

@@ -11,9 +11,6 @@ N = 1024
 PIECE = 256
 PER_COLUMN = 16
 
-WARM_UP = 4
-BANK = 512
-
 FLOPS = 2 * K * M * N
 
 
@@ -24,16 +21,11 @@ def tile_qnetwork_kernel(tc, table, v, gain, offs, out):
         nc.sync.dma_start(offsets[:], offs)
         weights = held.tile([K, M], BF16, name="weights")
         nc.scalar.dma_start(weights[:], v)
-        gain_col = held.tile([M, 1], F32, name="gain_col")
-        nc.scalar.dma_start(gain_col[:], gain)
         nodes = held.tile([K, S], BF16, name="nodes")
-        nc.sync.dma_start(nodes[:], table)
-
-        zeros = held.tile([K, M], BF16, name="zeros")
-        nc.vector.memset(zeros[:], 0.0)
-        unread = psum.tile([M, BANK], F32, name="unread")
-        for turn in range(WARM_UP):
-            nc.tensor.matmul(unread[:], zeros[:], zeros[:, 0:1].to_broadcast([K, BANK]), start=True, stop=True)
+        nc.sync.dma_start(nodes[:, 0 : S // 2], table[:, 0 : S // 2])
+        nc.scalar.dma_start(nodes[:, S // 2 : S], table[:, S // 2 : S])
+        gain_col = held.tile([M, 1], F32, name="gain_col")
+        nc.sync.dma_start(gain_col[:], gain)
 
         squares = held.tile([K, M], F32, name="squares")
         nc.vector.tensor_tensor(squares[:], weights[:], weights[:], MULT)

@@ -2,7 +2,7 @@ import concourse.mybir as mybir
 
 BF16, F32, U16 = mybir.dt.bfloat16, mybir.dt.float32, mybir.dt.uint16
 MULT, MAX = mybir.AluOpType.mult, mybir.AluOpType.max
-SQRT, RELU = mybir.ActivationFunctionType.Sqrt, mybir.ActivationFunctionType.Relu
+INVERSE_ROOT, RELU = mybir.ActivationFunctionType.Abs_reciprocal_sqrt, mybir.ActivationFunctionType.Relu
 
 K = 128
 M = 128
@@ -33,12 +33,10 @@ def tile_qnetwork_kernel(tc, table, v, gain, offs, out):
         nc.vector.memset(ones[:], 1.0)
         sum_squares = psum.tile([M, 1], F32, name="sum_squares")
         nc.tensor.matmul(sum_squares[:], squares[:], ones[:], start=True, stop=True)
-        length = held.tile([M, 1], F32, name="length")
-        nc.scalar.activation(length[:], sum_squares[:], SQRT)
         inverse_length = held.tile([M, 1], F32, name="inverse_length")
-        nc.vector.reciprocal(inverse_length[:], length[:])
+        nc.scalar.activation(inverse_length[:], sum_squares[:], INVERSE_ROOT)
         scale = held.tile([M, 1], F32, name="scale")
-        nc.vector.tensor_tensor(scale[:], inverse_length[:], gain_col[:], MULT)
+        nc.scalar.mul(scale[:], inverse_length[:], gain_col[:])
 
         for piece in range(N // PIECE):
             first = piece * PIECE

@@ -2,13 +2,14 @@ import concourse.mybir as mybir
 
 BF16, F32, U16 = mybir.dt.bfloat16, mybir.dt.float32, mybir.dt.uint16
 MULT, MAX = mybir.AluOpType.mult, mybir.AluOpType.max
-INVERSE_ROOT, RELU = mybir.ActivationFunctionType.Abs_reciprocal_sqrt, mybir.ActivationFunctionType.Relu
+SQRT, RELU = mybir.ActivationFunctionType.Sqrt, mybir.ActivationFunctionType.Relu
 
 K = 128
 M = 128
 S = 2048
 N = 1024
-PIECE = 256
+PIECE = 128
+BANKS = 8
 PER_COLUMN = 16
 
 FLOPS = 2 * K * M * N
@@ -16,16 +17,19 @@ FLOPS = 2 * K * M * N
 
 def tile_qnetwork_kernel(tc, table, v, gain, offs, out):
     nc = tc.nc
-    with tc.tile_pool(name="held", bufs=1) as held, tc.psum_pool(name="psum", bufs=1) as psum:
+    with (
+        tc.tile_pool(name="held", bufs=1) as held,
+        tc.psum_pool(name="psum", bufs=1) as psum,
+        tc.psum_pool(name="ring", bufs=BANKS - 1) as ring,
+    ):
         offsets = held.tile([K, N // PER_COLUMN], U16, name="offsets")
         nc.sync.dma_start(offsets[:], offs)
         weights = held.tile([K, M], BF16, name="weights")
         nc.scalar.dma_start(weights[:], v)
-        nodes = held.tile([K, S], BF16, name="nodes")
-        nc.sync.dma_start(nodes[:, 0 : S // 2], table[:, 0 : S // 2])
-        nc.scalar.dma_start(nodes[:, S // 2 : S], table[:, S // 2 : S])
         gain_col = held.tile([M, 1], F32, name="gain_col")
-        nc.sync.dma_start(gain_col[:], gain)
+        nc.scalar.dma_start(gain_col[:], gain)
+        nodes = held.tile([K, S], BF16, name="nodes")
+        nc.sync.dma_start(nodes[:], table)
 
         squares = held.tile([K, M], F32, name="squares")
         nc.vector.tensor_tensor(squares[:], weights[:], weights[:], MULT)
@@ -33,15 +37,17 @@ def tile_qnetwork_kernel(tc, table, v, gain, offs, out):
         nc.vector.memset(ones[:], 1.0)
         sum_squares = psum.tile([M, 1], F32, name="sum_squares")
         nc.tensor.matmul(sum_squares[:], squares[:], ones[:], start=True, stop=True)
+        length = held.tile([M, 1], F32, name="length")
+        nc.scalar.activation(length[:], sum_squares[:], SQRT)
         inverse_length = held.tile([M, 1], F32, name="inverse_length")
-        nc.scalar.activation(inverse_length[:], sum_squares[:], INVERSE_ROOT)
+        nc.vector.reciprocal(inverse_length[:], length[:])
         scale = held.tile([M, 1], F32, name="scale")
-        nc.scalar.mul(scale[:], inverse_length[:], gain_col[:])
+        nc.vector.tensor_tensor(scale[:], inverse_length[:], gain_col[:], MULT)
 
         for piece in range(N // PIECE):
             first = piece * PIECE
             looked_up = nodes[:].indirect(offsets[:, first // PER_COLUMN : (first + PIECE) // PER_COLUMN])
-            projected = psum.tile([M, PIECE], F32, name=f"projected{piece}")
+            projected = ring.tile([M, PIECE], F32, name="projected")
             nc.tensor.matmul(projected[:], weights[:], looked_up, start=True, stop=True)
             result = held.tile([M, PIECE], F32, name=f"result{piece}")
             if piece % 2 == 0:

@@ -8,8 +8,7 @@ K = 128
 M = 128
 S = 2048
 N = 1024
-PIECE = 128
-BANKS = 8
+PIECE = 256
 PER_COLUMN = 16
 
 FLOPS = 2 * K * M * N
@@ -17,19 +16,15 @@ FLOPS = 2 * K * M * N
 
 def tile_qnetwork_kernel(tc, table, v, gain, offs, out):
     nc = tc.nc
-    with (
-        tc.tile_pool(name="held", bufs=1) as held,
-        tc.psum_pool(name="psum", bufs=1) as psum,
-        tc.psum_pool(name="ring", bufs=BANKS - 1) as ring,
-    ):
+    with tc.tile_pool(name="held", bufs=1) as held, tc.psum_pool(name="psum", bufs=1) as psum:
+        nodes = held.tile([K, S], BF16, name="nodes")
+        nc.scalar.dma_start(nodes[:], table)
+        weights = held.tile([K, M], BF16, name="weights")
+        nc.sync.dma_start(weights[:], v)
         offsets = held.tile([K, N // PER_COLUMN], U16, name="offsets")
         nc.sync.dma_start(offsets[:], offs)
-        weights = held.tile([K, M], BF16, name="weights")
-        nc.scalar.dma_start(weights[:], v)
         gain_col = held.tile([M, 1], F32, name="gain_col")
-        nc.scalar.dma_start(gain_col[:], gain)
-        nodes = held.tile([K, S], BF16, name="nodes")
-        nc.sync.dma_start(nodes[:], table)
+        nc.sync.dma_start(gain_col[:], gain)
 
         squares = held.tile([K, M], F32, name="squares")
         nc.vector.tensor_tensor(squares[:], weights[:], weights[:], MULT)
@@ -47,12 +42,11 @@ def tile_qnetwork_kernel(tc, table, v, gain, offs, out):
         for piece in range(N // PIECE):
             first = piece * PIECE
             looked_up = nodes[:].indirect(offsets[:, first // PER_COLUMN : (first + PIECE) // PER_COLUMN])
-            projected = ring.tile([M, PIECE], F32, name="projected")
+            projected = psum.tile([M, PIECE], F32, name=f"projected{piece}")
             nc.tensor.matmul(projected[:], weights[:], looked_up, start=True, stop=True)
             result = held.tile([M, PIECE], F32, name=f"result{piece}")
             if piece % 2 == 0:
                 nc.scalar.activation(result[:], projected[:], RELU, scale=scale[:])
-                nc.scalar.dma_start(out[:, first : first + PIECE], result[:])
             else:
                 nc.vector.tensor_scalar(result[:], projected[:], scale[:], 0.0, MULT, MAX)
-                nc.sync.dma_start(out[:, first : first + PIECE], result[:])
+            nc.sync.dma_start(out[:, first : first + PIECE], result[:])

@@ -2,7 +2,7 @@ import concourse.mybir as mybir
 
 BF16, F32, U16 = mybir.dt.bfloat16, mybir.dt.float32, mybir.dt.uint16
 MULT, MAX = mybir.AluOpType.mult, mybir.AluOpType.max
-SQRT, RELU = mybir.ActivationFunctionType.Sqrt, mybir.ActivationFunctionType.Relu
+SQRT = mybir.ActivationFunctionType.Sqrt
 
 K = 128
 M = 128
@@ -45,8 +45,5 @@ def tile_qnetwork_kernel(tc, table, v, gain, offs, out):
             projected = psum.tile([M, PIECE], F32, name=f"projected{piece}")
             nc.tensor.matmul(projected[:], weights[:], looked_up, start=True, stop=True)
             result = held.tile([M, PIECE], F32, name=f"result{piece}")
-            if piece % 2 == 0:
-                nc.scalar.activation(result[:], projected[:], RELU, scale=scale[:])
-            else:
-                nc.vector.tensor_scalar(result[:], projected[:], scale[:], 0.0, MULT, MAX)
+            nc.vector.tensor_scalar(result[:], projected[:], scale[:], 0.0, MULT, MAX)
             nc.sync.dma_start(out[:, first : first + PIECE], result[:])

@@ -9,6 +9,7 @@ M = 128
 S = 2048
 N = 1024
 PIECE = 256
+DMA_BLOCK = 256
 PER_COLUMN = 16
 
 FLOPS = 2 * K * M * N
@@ -44,6 +45,6 @@ def tile_qnetwork_kernel(tc, table, v, gain, offs, out):
             looked_up = nodes[:].indirect(offsets[:, first // PER_COLUMN : (first + PIECE) // PER_COLUMN])
             projected = psum.tile([M, PIECE], F32, name=f"projected{piece}")
             nc.tensor.matmul(projected[:], weights[:], looked_up, start=True, stop=True)
-            result = held.tile([M, PIECE], F32, name=f"result{piece}")
+            result = held.tile([M, PIECE], F32, name=f"result{piece}", align_bytes=DMA_BLOCK)
             nc.vector.tensor_scalar(result[:], projected[:], scale[:], 0.0, MULT, MAX)
             nc.sync.dma_start(out[:, first : first + PIECE], result[:])

@@ -25,7 +25,7 @@ def tile_qnetwork_kernel(tc, table, v, gain, offs, out):
         offsets = held.tile([K, N // PER_COLUMN], U16, name="offsets")
         nc.sync.dma_start(offsets[:], offs)
         gain_col = held.tile([M, 1], F32, name="gain_col")
-        nc.sync.dma_start(gain_col[:], gain)
+        nc.scalar.dma_start(gain_col[:], gain)
 
         squares = held.tile([K, M], F32, name="squares")
         nc.vector.tensor_tensor(squares[:], weights[:], weights[:], MULT)

import concourse.mybir as mybir

BF16, F32, U16 = mybir.dt.bfloat16, mybir.dt.float32, mybir.dt.uint16
MULT, MAX = mybir.AluOpType.mult, mybir.AluOpType.max
SQRT = mybir.ActivationFunctionType.Sqrt

K = 128
M = 128
S = 2048
N = 1024
PIECE = 256
DMA_BLOCK = 256
PER_COLUMN = 16

FLOPS = 2 * K * M * N


def tile_qnetwork_kernel(tc, table, v, gain, offs, out):
    nc = tc.nc
    with tc.tile_pool(name="held", bufs=1) as held, tc.psum_pool(name="psum", bufs=1) as psum:
        nodes = held.tile([K, S], BF16, name="nodes")
        nc.scalar.dma_start(nodes[:], table)
        weights = held.tile([K, M], BF16, name="weights")
        nc.sync.dma_start(weights[:], v)
        offsets = held.tile([K, N // PER_COLUMN], U16, name="offsets")
        nc.sync.dma_start(offsets[:], offs)
        gain_col = held.tile([M, 1], F32, name="gain_col")
        nc.scalar.dma_start(gain_col[:], gain)

        squares = held.tile([K, M], F32, name="squares")
        nc.vector.tensor_tensor(squares[:], weights[:], weights[:], MULT)
        ones = held.tile([K, 1], F32, name="ones")
        nc.vector.memset(ones[:], 1.0)
        sum_squares = psum.tile([M, 1], F32, name="sum_squares")
        nc.tensor.matmul(sum_squares[:], squares[:], ones[:], start=True, stop=True)
        length = held.tile([M, 1], F32, name="length")
        nc.scalar.activation(length[:], sum_squares[:], SQRT)
        inverse_length = held.tile([M, 1], F32, name="inverse_length")
        nc.vector.reciprocal(inverse_length[:], length[:])
        scale = held.tile([M, 1], F32, name="scale")
        nc.vector.tensor_tensor(scale[:], inverse_length[:], gain_col[:], MULT)

        for piece in range(N // PIECE):
            first = piece * PIECE
            looked_up = nodes[:].indirect(offsets[:, first // PER_COLUMN : (first + PIECE) // PER_COLUMN])
            projected = psum.tile([M, PIECE], F32, name=f"projected{piece}")
            nc.tensor.matmul(projected[:], weights[:], looked_up, start=True, stop=True)
            result = held.tile([M, PIECE], F32, name=f"result{piece}", align_bytes=DMA_BLOCK)
            nc.vector.tensor_scalar(result[:], projected[:], scale[:], 0.0, MULT, MAX)
            nc.sync.dma_start(out[:, first : first + PIECE], result[:])
